import numpy as np
import ml_dtypes


def mxq(x, axis, fmt="e4m3"):
    dtype, down = {"e4m3": (ml_dtypes.float8_e4m3fn, 7), "e5m2": (ml_dtypes.float8_e5m2, 14)}[fmt]
    v = np.moveaxis(np.asarray(x, np.float32).astype(ml_dtypes.bfloat16).astype(np.float64), axis, -1)
    blocks = v.reshape(v.shape[:-1] + (-1, 32))
    amax = np.abs(blocks).max(-1, keepdims=True)
    byte = np.maximum(np.where(amax > 0, np.frexp(amax)[1] - 1 + 127, 0) - down, 1)
    scale = np.exp2(byte - 127.0)
    codes = (blocks / scale).astype(np.float32).astype(dtype).astype(np.float64)
    return np.moveaxis((codes * scale).reshape(v.shape), -1, axis)


WIDE = False


def mx_kscale(k):
    if not WIDE:
        return np.ones(k)
    levels = np.array([20, -20, 10, -10, 0])
    a = np.random.permutation(np.resize(levels, k // 512 * 4)).reshape(k // 512, 4)
    idx = np.arange(k)
    return np.exp2(a[idx // 512, idx % 128 // 32])


BF16 = ml_dtypes.bfloat16


def bf(x):
    return np.asarray(x, np.float32).astype(BF16)


def f64(x):
    return np.asarray(x).astype(np.float64)


BLOCK = 128
T, IN_F, OUT_F = 512, 3584, 3072


def block_scale(weight, scale, block_size=BLOCK):
    out_f, in_f = weight.shape
    ob, ib = out_f // block_size, in_f // block_size
    w = weight.reshape(ob, block_size, ib, block_size)
    w = w * scale[:, None, :, None]
    return w.reshape(out_f, in_f)


def setup_inputs():
    u = mx_kscale(OUT_F)
    x = np.random.standard_normal((T, IN_F))
    weight = np.random.standard_normal((OUT_F, IN_F)) * 0.02 / u[:, None]
    scale = np.random.uniform(0.5, 1.5, (OUT_F // BLOCK, IN_F // BLOCK))
    g = np.random.standard_normal((T, OUT_F)) * np.exp2(np.random.randint(-12, 1, (T, 1))) * 16.0 * u[None, :]
    return {"x": bf(x), "weight": bf(weight), "scale": bf(scale), "grad_out": bf(g)}


def reference(x, weight, scale, grad_out):
    w = block_scale(f64(weight), f64(scale))
    return mxq(f64(grad_out), 1, "e5m2") @ mxq(w, 0, "e4m3")

@@ -1,0 +1,211 @@
+from contextlib import ExitStack
+
+import concourse.mybir as mybir
+from concourse.masks import make_identity
+
+F32 = mybir.dt.float32
+BF16 = mybir.dt.bfloat16
+U32 = mybir.dt.uint32
+U8 = mybir.dt.uint8
+E4M3X4 = mybir.dt.float8_e4m3fn_x4
+E5M2X4 = mybir.dt.float8_e5m2_x4
+MULT = mybir.AluOpType.mult
+COPY = mybir.ActivationFunctionType.Copy
+
+P = 128
+T, IN_F, OUT_F = 512, 3584, 3072
+PASSES = OUT_F // 512
+M_TILES = T // P
+GAIN_COLS = IN_F // 128
+
+FLOPS = 2 * T * IN_F * OUT_F
+BYTES = 2 * OUT_F * IN_F + 2 * (OUT_F // 128) * GAIN_COLS + 2 * T * OUT_F + 4 * T * IN_F
+
+CHUNKS = ((0, 1024), (1024, 1024), (2048, 1024), (3072, 512))
+N_RAW = 6
+N_GRP = 3
+N_CODES = 5
+N_STAGE = 5
+SHARE_BIG = 4
+SHARE_SMALL = 2
+ZERO_STEPS = 2
+MANUAL = True
+
+
+def tile_fp8linear_kernel(tc, x, weight, scale, grad_out, out):
+    nc = tc.nc
+    pieces = [(j, c) for j in range(len(CHUNKS)) for c in range(PASSES)]
+    n_pieces = len(pieces)
+
+    with ExitStack() as ctx:
+        const = ctx.enter_context(tc.tile_pool(name="const", bufs=1))
+        rawp = ctx.enter_context(tc.tile_pool(name="rawp", bufs=N_RAW))
+        grpp = ctx.enter_context(tc.tile_pool(name="grpp", bufs=N_GRP))
+        codep = ctx.enter_context(tc.tile_pool(name="codep", bufs=N_CODES))
+        stagep = ctx.enter_context(tc.tile_pool(name="stagep", bufs=N_STAGE))
+        lastp = ctx.enter_context(tc.tile_pool(name="lastp", bufs=M_TILES))
+        psum = ctx.enter_context(tc.psum_pool(name="psum", bufs=1))
+        if MANUAL:
+            ctx.enter_context(tc.manual_schedule())
+
+        raw, grp, codes, planes, acc = {}, {}, {}, {}, {}
+
+        def bank(b, shape, name):
+            return psum.tile(shape, F32, tag="bank%d" % b, name=name)
+
+        def load(i):
+            if i >= n_pieces:
+                return
+            j, c = pieces[i]
+            col0, width = CHUNKS[j]
+            raw[i] = rawp.tile([P, 4, width], BF16, tag="raw", name="raw")
+            nc.sync.dma_start(
+                out=raw[i][:],
+                in_=weight[512 * c : 512 * (c + 1), col0 : col0 + width].rearrange("(p t) w -> p t w", t=4),
+            )
+
+        def scalar_share(i):
+            j, c = pieces[i]
+            if j > 0 and 1 <= c <= ZERO_STEPS:
+                return 0
+            return SHARE_BIG if CHUNKS[j][1] == 1024 else SHARE_SMALL
+
+        def regroup(i):
+            j, c = pieces[i]
+            col0, width = CHUNKS[j]
+            blocks = width // 128
+            grp[i] = grpp.tile([P, width, 4], BF16, tag="grp", name="grp", align_bytes=64)
+            for b in range(blocks):
+                cols = slice(128 * b, 128 * (b + 1))
+                src = raw[i][:, :, cols].rearrange("p t (a i) -> p a t i", i=4)
+                dst = grp[i][:, cols, :].rearrange("p (a i) t -> p a t i", i=4)
+                g = GAIN_COLS * c + col0 // 128 + b
+                if b < blocks - scalar_share(i):
+                    nc.vector.tensor_scalar(out=dst, in0=src, scalar1=gain[:, g : g + 1], scalar2=None, op0=MULT)
+                else:
+                    nc.scalar.activation(out=dst, in_=src, func=COPY, scale=gain[:, g : g + 1])
+
+        def quantise(i):
+            width = CHUNKS[pieces[i][0]][1]
+            codes[i] = codep.tile([P, width], U32, tag="codes", name="codes", align_bytes=64)
+            planes[i] = codep.tile([P, width], U8, tag="planes", name="planes", align_bytes=64)
+            nc.vector.quantize_mx(
+                out=codes[i][:].bitcast(E4M3X4),
+                scales=planes[i][:],
+                in_=grp[i][:].rearrange("p w t -> p (w t)"),
+            )
+
+        def group_order(j):
+            halves = CHUNKS[j][1] // 512
+            if j == len(CHUNKS) - 2:
+                return [(s, m) for s in range(halves) for m in range(M_TILES)]
+            return [(s, m) for m in range(M_TILES) for s in range(halves)]
+
+        def multiply(i):
+            j, c = pieces[i]
+            order = group_order(j) if c == PASSES - 1 else group_order(0)[:: 2 if CHUNKS[j][1] == 512 else 1]
+            for s, m in order:
+                if c == 0:
+                    acc[(s, m)] = bank(2 * m + s, [P, 512], "acc")
+                g_cols = slice(768 * m + 128 * c, 768 * m + 128 * (c + 1))
+                w_cols = slice(512 * s, 512 * (s + 1))
+                nc.tensor.matmul_mx(
+                    out=acc[(s, m)][:],
+                    lhsT=g_codes[:, g_cols].bitcast(E5M2X4),
+                    lhsT_scale=g_planes[:, g_cols],
+                    rhs=codes[i][:, w_cols].bitcast(E4M3X4),
+                    rhs_scale=planes[i][:, w_cols],
+                    start=(c == 0),
+                    stop=(c == PASSES - 1),
+                )
+
+        def evacuate(j):
+            col0, width = CHUNKS[j]
+            halves = width // 512
+            last = j == len(CHUNKS) - 1
+            stage, filled = {}, {}
+            for s, m in group_order(j):
+                if m not in stage:
+                    if last:
+                        stage[m] = lastp.tile([P, width], F32, tag="last", name="last")
+                    else:
+                        stage[m] = stagep.tile([P, width], F32, tag="stage", name="stage")
+                    filled[m] = 0
+                dst = stage[m][:, 512 * s : 512 * (s + 1)]
+                if last and m % 2 == 1:
+                    nc.vector.tensor_copy(out=dst, in_=acc[(s, m)][:])
+                else:
+                    nc.scalar.copy(out=dst, in_=acc[(s, m)][:])
+                filled[m] += 1
+                if filled[m] == halves:
+                    nc.sync.dma_start(out=out[P * m : P * (m + 1), col0 : col0 + width], in_=stage[m][:])
+
+        sel = const.tile([P, P], BF16, name="sel")
+        diag = const.tile([P, 256], BF16, name="diag")
+        gain = const.tile([P, PASSES * GAIN_COLS], F32, name="gain")
+        ident = const.tile([P, P], F32, name="ident")
+        g_codes = const.tile([P, M_TILES * 768], U32, name="g_codes", align_bytes=64)
+        g_planes = const.tile([P, M_TILES * 768], U8, name="g_planes", align_bytes=64)
+        nc.vector.memset(diag[:], 0.0)
+        nc.vector.memset(sel[:], 0.0)
+        for q in range(4):
+            nc.vector.memset(sel[32 * q : 32 * (q + 1), 32 * q : 32 * (q + 1)], 1.0)
+        for c in range(PASSES):
+            nc.scalar.dma_start(
+                out=diag[c:P:32, GAIN_COLS * c : GAIN_COLS * (c + 1)], in_=scale[4 * c : 4 * (c + 1), :]
+            )
+        make_identity(nc, ident[:])
+
+        load(0)
+        g_raw, g_grp = [], []
+        for m in range(M_TILES):
+            g_raw.append(const.tile([P, OUT_F], BF16, name="g_raw%d" % m))
+            g_grp.append(const.tile([P, OUT_F], BF16, name="g_grp%d" % m, align_bytes=64))
+            nc.sync.dma_start(out=g_raw[m][:], in_=grad_out[P * m : P * (m + 1), :])
+        for i in range(1, N_RAW):
+            load(i)
+
+        gain_ps = bank(7, [P, 256], "gain_ps")
+        nc.tensor.matmul(out=gain_ps[:], lhsT=sel[:], rhs=diag[:], start=True, stop=True)
+        nc.vector.tensor_copy(out=gain[:], in_=gain_ps[:, : PASSES * GAIN_COLS])
+
+        regroup(0)
+        load(N_RAW)
+
+        def quantise_g(m):
+            for lo, hi in ((0, 512), (512, 768)):
+                nc.vector.quantize_mx(
+                    out=g_codes[:, 768 * m + lo : 768 * m + hi].bitcast(E5M2X4),
+                    scales=g_planes[:, 768 * m + lo : 768 * m + hi],
+                    in_=g_grp[m][:, 4 * lo : 4 * hi],
+                )
+
+        for m in range(M_TILES):
+            words = g_raw[m][:].bitcast(F32)
+            grouped = g_grp[m][:].bitcast(F32).rearrange("p (c r u) -> p c r u", c=PASSES, r=P, u=2)
+            for b in range(PASSES // 2):
+                turned = bank((3 * m + b) % 8, [P, 2, 2, P], "turned")
+                for cc in range(2):
+                    for u in range(2):
+                        first = 256 * (2 * b + cc) + u
+                        nc.tensor.transpose(turned[:, cc, u, :], words[:, first : first + 255 : 2], ident[:])
+                dst = grouped[:, 2 * b : 2 * b + 2]
+                src = turned[:].rearrange("p c u r -> p c r u")
+                if (3 * m + b) % 2 == 0:
+                    nc.scalar.copy(out=dst, in_=src)
+                else:
+                    nc.vector.tensor_copy(out=dst, in_=src)
+            if m >= 1:
+                quantise_g(m - 1)
+        quantise_g(M_TILES - 1)
+
+        for i in range(1, n_pieces + 2):
+            if i < n_pieces:
+                regroup(i)
+                load(i + N_RAW)
+            if i - 1 < n_pieces:
+                quantise(i - 1)
+            if i - 2 >= 0:
+                multiply(i - 2)
+                if pieces[i - 2][1] == PASSES - 1:
+                    evacuate(pieces[i - 2][0])

@@ -22,13 +22,13 @@ FLOPS = 2 * T * IN_F * OUT_F
 BYTES = 2 * OUT_F * IN_F + 2 * (OUT_F // 128) * GAIN_COLS + 2 * T * OUT_F + 4 * T * IN_F
 
 CHUNKS = ((0, 1024), (1024, 1024), (2048, 1024), (3072, 512))
-N_RAW = 6
-N_GRP = 3
-N_CODES = 5
-N_STAGE = 5
-SHARE_BIG = 4
-SHARE_SMALL = 2
-ZERO_STEPS = 2
+N_RAW = 10
+N_GRP = 4
+N_CODES = 6
+N_STAGE = 8
+SHARES_FIRST = (4, 4, 4, 4, 4, 4)
+SHARES_BIG = (4, 2, 0, 4, 4, 4)
+SHARES_SMALL = (2, 2, 0, 0, 2, 2)
 MANUAL = True
 
 
@@ -66,9 +66,9 @@ def tile_fp8linear_kernel(tc, x, weight, scale, grad_out, out):
 
         def scalar_share(i):
             j, c = pieces[i]
-            if j > 0 and 1 <= c <= ZERO_STEPS:
-                return 0
-            return SHARE_BIG if CHUNKS[j][1] == 1024 else SHARE_SMALL
+            if CHUNKS[j][1] == 512:
+                return SHARES_SMALL[c]
+            return SHARES_FIRST[c] if j == 0 else SHARES_BIG[c]
 
         def regroup(i):
             j, c = pieces[i]
@@ -159,10 +159,9 @@ def tile_fp8linear_kernel(tc, x, weight, scale, grad_out, out):
         load(0)
         g_raw, g_grp = [], []
         for m in range(M_TILES):
-            g_raw.append(const.tile([P, OUT_F], BF16, name="g_raw%d" % m))
-            g_grp.append(const.tile([P, OUT_F], BF16, name="g_grp%d" % m, align_bytes=64))
+            g_raw.append(rawp.tile([P, OUT_F], BF16, tag="raw", name="g_raw"))
             nc.sync.dma_start(out=g_raw[m][:], in_=grad_out[P * m : P * (m + 1), :])
-        for i in range(1, N_RAW):
+        for i in range(1, N_RAW - M_TILES):
             load(i)
 
         gain_ps = bank(7, [P, 256], "gain_ps")
@@ -170,7 +169,7 @@ def tile_fp8linear_kernel(tc, x, weight, scale, grad_out, out):
         nc.vector.tensor_copy(out=gain[:], in_=gain_ps[:, : PASSES * GAIN_COLS])
 
         regroup(0)
-        load(N_RAW)
+        load(N_RAW - M_TILES)
 
         def quantise_g(m):
             for lo, hi in ((0, 512), (512, 768)):
@@ -181,6 +180,7 @@ def tile_fp8linear_kernel(tc, x, weight, scale, grad_out, out):
                 )
 
         for m in range(M_TILES):
+            g_grp.append(grpp.tile([P, OUT_F], BF16, tag="grp", name="g_grp", align_bytes=64))
             words = g_raw[m][:].bitcast(F32)
             grouped = g_grp[m][:].bitcast(F32).rearrange("p (c r u) -> p c r u", c=PASSES, r=P, u=2)
             for b in range(PASSES // 2):
@@ -195,7 +195,10 @@ def tile_fp8linear_kernel(tc, x, weight, scale, grad_out, out):
                     nc.scalar.copy(out=dst, in_=src)
                 else:
                     nc.vector.tensor_copy(out=dst, in_=src)
-            if m >= 1:
+            load(N_RAW - M_TILES + 1 + m)
+            if m == 0:
+                quantise(0)
+            else:
                 quantise_g(m - 1)
         quantise_g(M_TILES - 1)
 
@@ -203,7 +206,7 @@ def tile_fp8linear_kernel(tc, x, weight, scale, grad_out, out):
             if i < n_pieces:
                 regroup(i)
                 load(i + N_RAW)
-            if i - 1 < n_pieces:
+            if 1 <= i - 1 < n_pieces:
                 quantise(i - 1)
             if i - 2 >= 0:
                 multiply(i - 2)

@@ -29,7 +29,7 @@ N_STAGE = 8
 SHARES_FIRST = (4, 4, 4, 4, 4, 4)
 SHARES_BIG = (4, 2, 0, 4, 4, 4)
 SHARES_SMALL = (2, 2, 0, 0, 2, 2)
-MANUAL = True
+MANUAL = False
 
 
 def tile_fp8linear_kernel(tc, x, weight, scale, grad_out, out):

@@ -29,7 +29,7 @@ N_STAGE = 8
 SHARES_FIRST = (4, 4, 4, 4, 4, 4)
 SHARES_BIG = (4, 2, 0, 4, 4, 4)
 SHARES_SMALL = (2, 2, 0, 0, 2, 2)
-MANUAL = False
+MANUAL = True
 
 
 def tile_fp8linear_kernel(tc, x, weight, scale, grad_out, out):
@@ -158,10 +158,12 @@ def tile_fp8linear_kernel(tc, x, weight, scale, grad_out, out):
 
         load(0)
         g_raw, g_grp = [], []
-        for m in range(M_TILES):
-            g_raw.append(rawp.tile([P, OUT_F], BF16, tag="raw", name="g_raw"))
-            nc.sync.dma_start(out=g_raw[m][:], in_=grad_out[P * m : P * (m + 1), :])
-        for i in range(1, N_RAW - M_TILES):
+        for h in range(M_TILES // 2):
+            g_raw.append(const.tile([P, 2, OUT_F], BF16, name="g_raw%d" % h))
+            nc.sync.dma_start(
+                out=g_raw[h][:], in_=grad_out[2 * P * h : 2 * P * (h + 1), :].rearrange("(m p) k -> p m k", p=P)
+            )
+        for i in range(1, N_RAW):
             load(i)
 
         gain_ps = bank(7, [P, 256], "gain_ps")
@@ -169,7 +171,7 @@ def tile_fp8linear_kernel(tc, x, weight, scale, grad_out, out):
         nc.vector.tensor_copy(out=gain[:], in_=gain_ps[:, : PASSES * GAIN_COLS])
 
         regroup(0)
-        load(N_RAW - M_TILES)
+        load(N_RAW)
 
         def quantise_g(m):
             for lo, hi in ((0, 512), (512, 768)):
@@ -181,7 +183,7 @@ def tile_fp8linear_kernel(tc, x, weight, scale, grad_out, out):
 
         for m in range(M_TILES):
             g_grp.append(grpp.tile([P, OUT_F], BF16, tag="grp", name="g_grp", align_bytes=64))
-            words = g_raw[m][:].bitcast(F32)
+            words = g_raw[m // 2][:, m % 2, :].bitcast(F32)
             grouped = g_grp[m][:].bitcast(F32).rearrange("p (c r u) -> p c r u", c=PASSES, r=P, u=2)
             for b in range(PASSES // 2):
                 turned = bank((3 * m + b) % 8, [P, 2, 2, P], "turned")
@@ -195,7 +197,6 @@ def tile_fp8linear_kernel(tc, x, weight, scale, grad_out, out):
                     nc.scalar.copy(out=dst, in_=src)
                 else:
                     nc.vector.tensor_copy(out=dst, in_=src)
-            load(N_RAW - M_TILES + 1 + m)
             if m == 0:
                 quantise(0)
             else:

from contextlib import ExitStack

import concourse.mybir as mybir
from concourse.masks import make_identity

F32 = mybir.dt.float32
BF16 = mybir.dt.bfloat16
U32 = mybir.dt.uint32
U8 = mybir.dt.uint8
E4M3X4 = mybir.dt.float8_e4m3fn_x4
E5M2X4 = mybir.dt.float8_e5m2_x4
MULT = mybir.AluOpType.mult
COPY = mybir.ActivationFunctionType.Copy

P = 128
T, IN_F, OUT_F = 512, 3584, 3072
PASSES = OUT_F // 512
M_TILES = T // P
GAIN_COLS = IN_F // 128

FLOPS = 2 * T * IN_F * OUT_F
BYTES = 2 * OUT_F * IN_F + 2 * (OUT_F // 128) * GAIN_COLS + 2 * T * OUT_F + 4 * T * IN_F

CHUNKS = ((0, 1024), (1024, 1024), (2048, 1024), (3072, 512))
N_RAW = 10
N_GRP = 4
N_CODES = 6
N_STAGE = 8
SHARES_FIRST = (4, 4, 4, 4, 4, 4)
SHARES_BIG = (4, 2, 0, 4, 4, 4)
SHARES_SMALL = (2, 2, 0, 0, 2, 2)
MANUAL = True


def tile_fp8linear_kernel(tc, x, weight, scale, grad_out, out):
    nc = tc.nc
    pieces = [(j, c) for j in range(len(CHUNKS)) for c in range(PASSES)]
    n_pieces = len(pieces)

    with ExitStack() as ctx:
        const = ctx.enter_context(tc.tile_pool(name="const", bufs=1))
        rawp = ctx.enter_context(tc.tile_pool(name="rawp", bufs=N_RAW))
        grpp = ctx.enter_context(tc.tile_pool(name="grpp", bufs=N_GRP))
        codep = ctx.enter_context(tc.tile_pool(name="codep", bufs=N_CODES))
        stagep = ctx.enter_context(tc.tile_pool(name="stagep", bufs=N_STAGE))
        lastp = ctx.enter_context(tc.tile_pool(name="lastp", bufs=M_TILES))
        psum = ctx.enter_context(tc.psum_pool(name="psum", bufs=1))
        if MANUAL:
            ctx.enter_context(tc.manual_schedule())

        raw, grp, codes, planes, acc = {}, {}, {}, {}, {}

        def bank(b, shape, name):
            return psum.tile(shape, F32, tag="bank%d" % b, name=name)

        def load(i):
            if i >= n_pieces:
                return
            j, c = pieces[i]
            col0, width = CHUNKS[j]
            raw[i] = rawp.tile([P, 4, width], BF16, tag="raw", name="raw")
            nc.sync.dma_start(
                out=raw[i][:],
                in_=weight[512 * c : 512 * (c + 1), col0 : col0 + width].rearrange("(p t) w -> p t w", t=4),
            )

        def scalar_share(i):
            j, c = pieces[i]
            if CHUNKS[j][1] == 512:
                return SHARES_SMALL[c]
            return SHARES_FIRST[c] if j == 0 else SHARES_BIG[c]

        def regroup(i):
            j, c = pieces[i]
            col0, width = CHUNKS[j]
            blocks = width // 128
            grp[i] = grpp.tile([P, width, 4], BF16, tag="grp", name="grp", align_bytes=64)
            for b in range(blocks):
                cols = slice(128 * b, 128 * (b + 1))
                src = raw[i][:, :, cols].rearrange("p t (a i) -> p a t i", i=4)
                dst = grp[i][:, cols, :].rearrange("p (a i) t -> p a t i", i=4)
                g = GAIN_COLS * c + col0 // 128 + b
                if b < blocks - scalar_share(i):
                    nc.vector.tensor_scalar(out=dst, in0=src, scalar1=gain[:, g : g + 1], scalar2=None, op0=MULT)
                else:
                    nc.scalar.activation(out=dst, in_=src, func=COPY, scale=gain[:, g : g + 1])

        def quantise(i):
            width = CHUNKS[pieces[i][0]][1]
            codes[i] = codep.tile([P, width], U32, tag="codes", name="codes", align_bytes=64)
            planes[i] = codep.tile([P, width], U8, tag="planes", name="planes", align_bytes=64)
            nc.vector.quantize_mx(
                out=codes[i][:].bitcast(E4M3X4),
                scales=planes[i][:],
                in_=grp[i][:].rearrange("p w t -> p (w t)"),
            )

        def group_order(j):
            halves = CHUNKS[j][1] // 512
            if j == len(CHUNKS) - 2:
                return [(s, m) for s in range(halves) for m in range(M_TILES)]
            return [(s, m) for m in range(M_TILES) for s in range(halves)]

        def multiply(i):
            j, c = pieces[i]
            order = group_order(j) if c == PASSES - 1 else group_order(0)[:: 2 if CHUNKS[j][1] == 512 else 1]
            for s, m in order:
                if c == 0:
                    acc[(s, m)] = bank(2 * m + s, [P, 512], "acc")
                g_cols = slice(768 * m + 128 * c, 768 * m + 128 * (c + 1))
                w_cols = slice(512 * s, 512 * (s + 1))
                nc.tensor.matmul_mx(
                    out=acc[(s, m)][:],
                    lhsT=g_codes[:, g_cols].bitcast(E5M2X4),
                    lhsT_scale=g_planes[:, g_cols],
                    rhs=codes[i][:, w_cols].bitcast(E4M3X4),
                    rhs_scale=planes[i][:, w_cols],
                    start=(c == 0),
                    stop=(c == PASSES - 1),
                )

        def evacuate(j):
            col0, width = CHUNKS[j]
            halves = width // 512
            last = j == len(CHUNKS) - 1
            stage, filled = {}, {}
            for s, m in group_order(j):
                if m not in stage:
                    if last:
                        stage[m] = lastp.tile([P, width], F32, tag="last", name="last")
                    else:
                        stage[m] = stagep.tile([P, width], F32, tag="stage", name="stage")
                    filled[m] = 0
                dst = stage[m][:, 512 * s : 512 * (s + 1)]
                if last and m % 2 == 1:
                    nc.vector.tensor_copy(out=dst, in_=acc[(s, m)][:])
                else:
                    nc.scalar.copy(out=dst, in_=acc[(s, m)][:])
                filled[m] += 1
                if filled[m] == halves:
                    nc.sync.dma_start(out=out[P * m : P * (m + 1), col0 : col0 + width], in_=stage[m][:])

        sel = const.tile([P, P], BF16, name="sel")
        diag = const.tile([P, 256], BF16, name="diag")
        gain = const.tile([P, PASSES * GAIN_COLS], F32, name="gain")
        ident = const.tile([P, P], F32, name="ident")
        g_codes = const.tile([P, M_TILES * 768], U32, name="g_codes", align_bytes=64)
        g_planes = const.tile([P, M_TILES * 768], U8, name="g_planes", align_bytes=64)
        nc.vector.memset(diag[:], 0.0)
        nc.vector.memset(sel[:], 0.0)
        for q in range(4):
            nc.vector.memset(sel[32 * q : 32 * (q + 1), 32 * q : 32 * (q + 1)], 1.0)
        for c in range(PASSES):
            nc.scalar.dma_start(
                out=diag[c:P:32, GAIN_COLS * c : GAIN_COLS * (c + 1)], in_=scale[4 * c : 4 * (c + 1), :]
            )
        make_identity(nc, ident[:])

        load(0)
        g_raw, g_grp = [], []
        for h in range(M_TILES // 2):
            g_raw.append(const.tile([P, 2, OUT_F], BF16, name="g_raw%d" % h))
            nc.sync.dma_start(
                out=g_raw[h][:], in_=grad_out[2 * P * h : 2 * P * (h + 1), :].rearrange("(m p) k -> p m k", p=P)
            )
        for i in range(1, N_RAW):
            load(i)

        gain_ps = bank(7, [P, 256], "gain_ps")
        nc.tensor.matmul(out=gain_ps[:], lhsT=sel[:], rhs=diag[:], start=True, stop=True)
        nc.vector.tensor_copy(out=gain[:], in_=gain_ps[:, : PASSES * GAIN_COLS])

        regroup(0)
        load(N_RAW)

        def quantise_g(m):
            for lo, hi in ((0, 512), (512, 768)):
                nc.vector.quantize_mx(
                    out=g_codes[:, 768 * m + lo : 768 * m + hi].bitcast(E5M2X4),
                    scales=g_planes[:, 768 * m + lo : 768 * m + hi],
                    in_=g_grp[m][:, 4 * lo : 4 * hi],
                )

        for m in range(M_TILES):
            g_grp.append(grpp.tile([P, OUT_F], BF16, tag="grp", name="g_grp", align_bytes=64))
            words = g_raw[m // 2][:, m % 2, :].bitcast(F32)
            grouped = g_grp[m][:].bitcast(F32).rearrange("p (c r u) -> p c r u", c=PASSES, r=P, u=2)
            for b in range(PASSES // 2):
                turned = bank((3 * m + b) % 8, [P, 2, 2, P], "turned")
                for cc in range(2):
                    for u in range(2):
                        first = 256 * (2 * b + cc) + u
                        nc.tensor.transpose(turned[:, cc, u, :], words[:, first : first + 255 : 2], ident[:])
                dst = grouped[:, 2 * b : 2 * b + 2]
                src = turned[:].rearrange("p c u r -> p c r u")
                if (3 * m + b) % 2 == 0:
                    nc.scalar.copy(out=dst, in_=src)
                else:
                    nc.vector.tensor_copy(out=dst, in_=src)
            if m == 0:
                quantise(0)
            else:
                quantise_g(m - 1)
        quantise_g(M_TILES - 1)

        for i in range(1, n_pieces + 2):
            if i < n_pieces:
                regroup(i)
                load(i + N_RAW)
            if 1 <= i - 1 < n_pieces:
                quantise(i - 1)
            if i - 2 >= 0:
                multiply(i - 2)
                if pieces[i - 2][1] == PASSES - 1:
                    evacuate(pieces[i - 2][0])
